import numpy as np
import ml_dtypes


def mxq(x, axis, fmt="e4m3"):
    dtype, down = {"e4m3": (ml_dtypes.float8_e4m3fn, 7), "e5m2": (ml_dtypes.float8_e5m2, 14)}[fmt]
    v = np.moveaxis(np.asarray(x, np.float32).astype(ml_dtypes.bfloat16).astype(np.float64), axis, -1)
    blocks = v.reshape(v.shape[:-1] + (-1, 32))
    amax = np.abs(blocks).max(-1, keepdims=True)
    byte = np.maximum(np.where(amax > 0, np.frexp(amax)[1] - 1 + 127, 0) - down, 1)
    scale = np.exp2(byte - 127.0)
    codes = (blocks / scale).astype(np.float32).astype(dtype).astype(np.float64)
    return np.moveaxis((codes * scale).reshape(v.shape), -1, axis)


WIDE = False


def mx_kscale(k):
    if not WIDE:
        return np.ones(k)
    levels = np.array([10, -10, 5, -5, 0])
    if k % 512:
        return np.exp2(np.random.permutation(np.resize(levels, k // 32))).repeat(32)
    a = np.empty((k // 512, 16))
    for p in range(k // 512):
        a[p, :8] = np.random.permutation(np.resize(levels, 8))
        for g in range(8):
            far = levels[np.abs(levels - a[p, g]) >= 10]
            a[p, g + 8] = far[np.random.randint(len(far))]
    return np.exp2(a.ravel()).repeat(32)


BF16 = ml_dtypes.bfloat16


def bf(x):
    return np.asarray(x, np.float32).astype(BF16)


def f64(x):
    return np.asarray(x).astype(np.float64)


N, T, B, C, H = 256, 4, 8, 512, 128
N3 = T * N
O = H + H


def sigmoid(v):
    return 1.0 / (1.0 + np.exp(-v))


def setup_inputs():
    s, t = mx_kscale(N3), mx_kscale(C)
    return {"x": bf(np.random.standard_normal((N3, B, C)) * s[:, None, None] * t[None, None, :]),
            "A": bf(np.random.standard_normal((N3, N3)) / np.sqrt(N3) / s[None, :]),
            "W0": bf(np.random.standard_normal((O, C)) / np.sqrt(C) / t[None, :]),
            "b0": bf(np.random.standard_normal(O) * 0.3)}


def reference(x, A, W0, b0):
    h = f64(x).transpose(1, 2, 0)
    g = mxq(h, 2, "e4m3") @ mxq(f64(A), 1, "e4m3").T
    y = (mxq(f64(W0), 1, "e4m3") @ mxq(g, 1, "e4m3")) + f64(b0)[None, :, None]
    h1 = y[:, :H] * sigmoid(y[:, H:])
    return h1.transpose(2, 0, 1)

@@ -1,0 +1,275 @@
+from contextlib import ExitStack
+
+import concourse.mybir as mybir
+from concourse.masks import make_identity
+
+F32 = mybir.dt.float32
+BF16 = mybir.dt.bfloat16
+U32 = mybir.dt.uint32
+U8 = mybir.dt.uint8
+FP8X4 = mybir.dt.float8_e4m3fn_x4
+ACT = mybir.ActivationFunctionType
+ALU = mybir.AluOpType
+
+P = 128
+PACK = 4
+RUN = 8
+NODES = 1024
+BATCH = 8
+CHANNELS = 512
+HIDDEN = 128
+
+PASSES = NODES // (P * PACK)
+HALF = 512
+HALVES = NODES // HALF
+BLOCKS = HALF // P
+UNITS = BATCH * HALVES
+PIECES = BATCH * PASSES
+
+FLOPS = 2 * BATCH * CHANNELS * NODES * NODES + 2 * BATCH * 2 * HIDDEN * CHANNELS * NODES
+
+
+def tile_stsgcm_pa_t_kernel(tc, x, A, W0, b0, out):
+    nc = tc.nc
+    with ExitStack() as ctx:
+        ctx.enter_context(tc.manual_schedule())
+
+        const = ctx.enter_context(tc.tile_pool(name="const", bufs=1))
+        x_keep = ctx.enter_context(tc.tile_pool(name="x_keep", bufs=PIECES))
+        a_load = ctx.enter_context(tc.tile_pool(name="a_load", bufs=HALVES * BLOCKS))
+        a_keep = ctx.enter_context(tc.tile_pool(name="a_keep", bufs=HALVES * BLOCKS))
+        x_stage = ctx.enter_context(tc.tile_pool(name="x_stage", bufs=3))
+        g_stage = ctx.enter_context(tc.tile_pool(name="g_stage", bufs=3))
+        glu = ctx.enter_context(tc.tile_pool(name="glu", bufs=4))
+        psum_g = ctx.enter_context(tc.psum_pool(name="psum_g", bufs=4))
+        psum_y = ctx.enter_context(tc.psum_pool(name="psum_y", bufs=2))
+        psum_t = ctx.enter_context(tc.psum_pool(name="psum_t", bufs=2))
+
+        ident_f32 = const.tile([P, P], F32)
+        make_identity(nc, ident_f32[:])
+        ident_bf16 = const.tile([P, P], BF16)
+        make_identity(nc, ident_bf16[:])
+        bias_rows = const.tile([P, P], BF16)
+        nc.vector.memset(bias_rows[:], 0.0)
+        zero_col = const.tile([P, 1], F32)
+        nc.vector.memset(zero_col[:], 0.0)
+        half_col = const.tile([P, 1], F32)
+        nc.scalar.activation(out=half_col[:], in_=zero_col[:], func=ACT.Sigmoid)
+
+        w_raw = const.tile([P, 2, CHANNELS], BF16)
+        nc.sync.dma_start(out=w_raw[:], in_=W0.rearrange("(h o) c -> o h c", h=2))
+        nc.sync.dma_start(out=bias_rows[0:2, :], in_=b0.rearrange("(h j) -> h j", h=2))
+
+        x_raw = {}
+
+        def load_x(b):
+            for s in range(PASSES):
+                x_piece = x_keep.tile([P, PACK, CHANNELS], BF16)
+                nc.sync.dma_start(
+                    out=x_piece[:],
+                    in_=x[s * P * PACK : (s + 1) * P * PACK, b, :].rearrange("(p t) c -> p t c", t=PACK),
+                )
+                x_raw[PASSES * b + s] = x_piece
+
+        load_x(0)
+        a_raw = []
+        for block in range(HALVES * BLOCKS):
+            a_rows = a_load.tile([P, NODES], BF16)
+            nc.sync.dma_start(out=a_rows[:], in_=A[block * P : (block + 1) * P, :])
+            a_raw.append(a_rows)
+        for b in range(1, BATCH):
+            load_x(b)
+
+        w_slots = const.tile([P, 2, PACK, P], BF16)
+        for h in range(2):
+            nc.vector.tensor_copy(
+                out=w_slots[:, h].rearrange("p t (q i) -> p t q i", i=RUN),
+                in_=w_raw[:, h].rearrange("p (q t i) -> p t q i", t=PACK, i=RUN),
+            )
+        w_grouped = const.tile([P, 2 * HIDDEN, PACK], BF16, align_bytes=64)
+        for h in range(2):
+            w_bank = psum_t.tile([P, PACK, P], BF16, tag="t")
+            for t in range(PACK):
+                nc.tensor.transpose(
+                    out=w_bank[:, t, :], in_=w_slots[:, h, t, :], identity=ident_bf16[:]
+                )
+            nc.vector.tensor_copy(
+                out=w_grouped[:, h * HIDDEN : (h + 1) * HIDDEN, :],
+                in_=w_bank[:].rearrange("p t o -> p o t"),
+            )
+        bias_bank = psum_y.tile([P, P], BF16, tag="y")
+        nc.tensor.transpose(out=bias_bank[:], in_=bias_rows[:], identity=ident_bf16[:])
+        bias = const.tile([P, 2], F32)
+        nc.vector.tensor_copy(out=bias[:], in_=bias_bank[:, 0:2])
+        w_codes = const.tile([P, 2 * HIDDEN], U32, align_bytes=64)
+        w_scales = const.tile([P, 2 * HIDDEN], U8, align_bytes=64)
+        nc.vector.quantize_mx(
+            out=w_codes[:].bitcast(FP8X4),
+            scales=w_scales[:],
+            in_=w_grouped[:].rearrange("p o t -> p (o t)"),
+        )
+
+        x_grouped = {}
+        x_codes = {}
+        x_scales = {}
+
+        def regroup_x(piece):
+            grouped = x_stage.tile([P, CHANNELS, PACK], BF16, align_bytes=64)
+            nc.vector.tensor_copy(
+                out=grouped[:].rearrange("p (t q i) j -> p t q j i", t=PACK, i=RUN),
+                in_=x_raw[piece][:].rearrange("p j (q t i) -> p t q j i", t=PACK, i=RUN),
+            )
+            x_grouped[piece] = grouped
+
+        def quantise_x(piece):
+            b, s = divmod(piece, PASSES)
+            if s == 0:
+                codes = x_stage.tile([P, PASSES, CHANNELS], U32, align_bytes=64)
+                scales = x_stage.tile([P, PASSES, CHANNELS], U8, align_bytes=64)
+                x_codes[b] = codes
+                x_scales[b] = scales
+            nc.vector.quantize_mx(
+                out=x_codes[b][:, s, :].bitcast(FP8X4),
+                scales=x_scales[b][:, s, :],
+                in_=x_grouped[piece][:].rearrange("p c t -> p (c t)"),
+            )
+
+        a_codes = {}
+        a_scales = {}
+
+        def prepare_a(half):
+            for block in range(half * BLOCKS, (half + 1) * BLOCKS):
+                a_words = a_raw[block][:].bitcast(F32)
+                a_bank = psum_g.tile([P, PASSES * 2, P], F32, tag="g")
+                for su in range(PASSES * 2):
+                    s, u = divmod(su, 2)
+                    nc.tensor.transpose(
+                        out=a_bank[:, su, :],
+                        in_=a_words[:, s * 2 * P + u : (s + 1) * 2 * P : 2],
+                        identity=ident_f32[:],
+                    )
+                a_grouped = a_keep.tile([P, PASSES * P * PACK], BF16, align_bytes=64)
+                nc.scalar.copy(
+                    out=a_grouped[:].bitcast(F32).rearrange("p (s v u) -> p s v u", s=PASSES, u=2),
+                    in_=a_bank[:].rearrange("p (s u) v -> p s v u", u=2),
+                )
+                codes = a_keep.tile([P, PASSES, P], U32, align_bytes=64)
+                scales = a_keep.tile([P, PASSES, P], U8, align_bytes=64)
+                nc.vector.quantize_mx(
+                    out=codes[:].rearrange("p s v -> p (s v)").bitcast(FP8X4),
+                    scales=scales[:].rearrange("p s v -> p (s v)"),
+                    in_=a_grouped[:],
+                )
+                a_codes[block] = codes
+                a_scales[block] = scales
+
+        g_grouped = {}
+        g_codes = {}
+        g_scales = {}
+        gated = {}
+
+        def stage1(unit):
+            b, half = divmod(unit, HALVES)
+            grouped = g_stage.tile([P, HALF, PACK], BF16, align_bytes=64)
+            for k in range(BLOCKS):
+                g_bank = psum_g.tile([P, PACK, P], F32, tag="g")
+                for t in range(PACK):
+                    for s in range(PASSES):
+                        nc.tensor.matmul_mx(
+                            out=g_bank[:, t, :],
+                            lhsT=x_codes[b][:, s, t * P : (t + 1) * P].bitcast(FP8X4),
+                            lhsT_scale=x_scales[b][:, s, t * P : (t + 1) * P],
+                            rhs=a_codes[half * BLOCKS + k][:, s, :].bitcast(FP8X4),
+                            rhs_scale=a_scales[half * BLOCKS + k][:, s, :],
+                            start=(s == 0),
+                            stop=(s == PASSES - 1),
+                        )
+                nc.scalar.copy(
+                    out=grouped[:, k * P : (k + 1) * P, :], in_=g_bank[:].rearrange("p t v -> p v t")
+                )
+            g_grouped[unit] = grouped
+
+        def quantise_g(unit):
+            codes = g_stage.tile([P, HALF], U32, align_bytes=64)
+            scales = g_stage.tile([P, HALF], U8, align_bytes=64)
+            nc.vector.quantize_mx(
+                out=codes[:].bitcast(FP8X4),
+                scales=scales[:],
+                in_=g_grouped[unit][:].rearrange("p v t -> p (v t)"),
+            )
+            g_codes[unit] = codes
+            g_scales[unit] = scales
+
+        def stage2(unit):
+            y_banks = []
+            for h in (1, 0):
+                y_bank = psum_y.tile([P, HALF], F32, tag="y")
+                nc.tensor.matmul_mx(
+                    out=y_bank[:],
+                    lhsT=w_codes[:, h * HIDDEN : (h + 1) * HIDDEN].bitcast(FP8X4),
+                    lhsT_scale=w_scales[:, h * HIDDEN : (h + 1) * HIDDEN],
+                    rhs=g_codes[unit][:].bitcast(FP8X4),
+                    rhs_scale=g_scales[unit][:],
+                    start=True,
+                    stop=True,
+                )
+                y_banks.append(y_bank)
+            gate_bank, value_bank = y_banks
+            sig = glu.tile([P, HALF], F32)
+            nc.scalar.activation(
+                out=sig[:], in_=gate_bank[:], func=ACT.Sigmoid, bias=bias[:, 1:2], scale=1.0
+            )
+            product = glu.tile([P, HALF], F32)
+            nc.vector.scalar_tensor_tensor(
+                out=product[:],
+                in0=value_bank[:],
+                scalar=bias[:, 0:1],
+                in1=sig[:],
+                op0=ALU.add,
+                op1=ALU.mult,
+            )
+            gated[unit] = product
+
+        def write_out(b):
+            t_banks = []
+            for half in range(HALVES):
+                t_bank = psum_t.tile([P, BLOCKS, HIDDEN], F32, tag="t")
+                for k in range(BLOCKS):
+                    nc.tensor.transpose(
+                        out=t_bank[:, k, :],
+                        in_=gated[HALVES * b + half][:, k * P : (k + 1) * P],
+                        identity=ident_f32[:],
+                    )
+                t_banks.append(t_bank)
+            for half in range(HALVES):
+                result = glu.tile([P, BLOCKS, HIDDEN], F32)
+                if half == 0:
+                    nc.vector.tensor_copy(out=result[:], in_=t_banks[half][:])
+                else:
+                    nc.scalar.copy(out=result[:], in_=t_banks[half][:])
+                nc.sync.dma_start(
+                    out=out[half * HALF : (half + 1) * HALF, b, :].rearrange("(k p) j -> p k j", p=P),
+                    in_=result[:],
+                )
+
+        regroup_x(0)
+        regroup_x(1)
+        quantise_x(0)
+        quantise_x(1)
+        for half in range(HALVES):
+            prepare_a(half)
+        regroup_x(2)
+
+        for step in range(UNITS + 2):
+            if step < UNITS:
+                stage1(step)
+            if step + 2 < PIECES:
+                quantise_x(step + 2)
+            if step + 3 < PIECES:
+                regroup_x(step + 3)
+            if step < UNITS:
+                quantise_g(step)
+            if 1 <= step <= UNITS:
+                stage2(step - 1)
+            if step >= 3 and step % 2 == 1:
+                write_out((step - 3) // 2)

@@ -13,6 +13,7 @@ ALU = mybir.AluOpType
 
 P = 128
 PACK = 4
+SQ = 32
 RUN = 8
 NODES = 1024
 BATCH = 8
@@ -168,89 +169,107 @@ def tile_stsgcm_pa_t_kernel(tc, x, A, W0, b0, out):
         g_scales = {}
         gated = {}
 
-        def stage1(unit):
+        def stage1(unit, k, engine):
             b, half = divmod(unit, HALVES)
-            grouped = g_stage.tile([P, HALF, PACK], BF16, align_bytes=64)
-            for k in range(BLOCKS):
-                g_bank = psum_g.tile([P, PACK, P], F32, tag="g")
-                for t in range(PACK):
-                    for s in range(PASSES):
-                        nc.tensor.matmul_mx(
-                            out=g_bank[:, t, :],
-                            lhsT=x_codes[b][:, s, t * P : (t + 1) * P].bitcast(FP8X4),
-                            lhsT_scale=x_scales[b][:, s, t * P : (t + 1) * P],
-                            rhs=a_codes[half * BLOCKS + k][:, s, :].bitcast(FP8X4),
-                            rhs_scale=a_scales[half * BLOCKS + k][:, s, :],
-                            start=(s == 0),
-                            stop=(s == PASSES - 1),
-                        )
-                nc.scalar.copy(
-                    out=grouped[:, k * P : (k + 1) * P, :], in_=g_bank[:].rearrange("p t v -> p v t")
-                )
-            g_grouped[unit] = grouped
+            if k == 0:
+                grouped = g_stage.tile([P, HALF, PACK], BF16, align_bytes=64)
+                g_grouped[unit] = grouped
+            g_bank = psum_g.tile([P, PACK, P], F32, tag="g")
+            for t in range(PACK):
+                for s in range(PASSES):
+                    nc.tensor.matmul_mx(
+                        out=g_bank[:, t, :],
+                        lhsT=x_codes[b][:, s, t * P : (t + 1) * P].bitcast(FP8X4),
+                        lhsT_scale=x_scales[b][:, s, t * P : (t + 1) * P],
+                        rhs=a_codes[half * BLOCKS + k][:, s, :].bitcast(FP8X4),
+                        rhs_scale=a_scales[half * BLOCKS + k][:, s, :],
+                        start=(s == 0),
+                        stop=(s == PASSES - 1),
+                    )
+            copy(engine, g_grouped[unit][:, k * P : (k + 1) * P, :], g_bank[:].rearrange("p t v -> p v t"))
 
-        def quantise_g(unit):
-            codes = g_stage.tile([P, HALF], U32, align_bytes=64)
-            scales = g_stage.tile([P, HALF], U8, align_bytes=64)
+        def copy(engine, out_ap, in_ap):
+            if engine == "V":
+                nc.vector.tensor_copy(out=out_ap, in_=in_ap)
+            else:
+                nc.scalar.copy(out=out_ap, in_=in_ap)
+
+        def quantise_g(unit, first=0, last=BLOCKS):
+            if first == 0:
+                codes = g_stage.tile([P, HALF], U32, align_bytes=64)
+                scales = g_stage.tile([P, HALF], U8, align_bytes=64)
+                g_codes[unit] = codes
+                g_scales[unit] = scales
+            cols = slice(first * P, last * P)
             nc.vector.quantize_mx(
-                out=codes[:].bitcast(FP8X4),
-                scales=scales[:],
-                in_=g_grouped[unit][:].rearrange("p v t -> p (v t)"),
+                out=g_codes[unit][:, cols].bitcast(FP8X4),
+                scales=g_scales[unit][:, cols],
+                in_=g_grouped[unit][:, cols, :].rearrange("p v t -> p (v t)"),
             )
-            g_codes[unit] = codes
-            g_scales[unit] = scales
 
-        def stage2(unit):
+        def stage2(unit, first=0, last=BLOCKS, pool=psum_y, tag="y"):
+            cols = slice(first * P, last * P)
             y_banks = []
             for h in (1, 0):
-                y_bank = psum_y.tile([P, HALF], F32, tag="y")
+                y_bank = pool.tile([P, (last - first) * P], F32, tag=tag)
                 nc.tensor.matmul_mx(
                     out=y_bank[:],
                     lhsT=w_codes[:, h * HIDDEN : (h + 1) * HIDDEN].bitcast(FP8X4),
                     lhsT_scale=w_scales[:, h * HIDDEN : (h + 1) * HIDDEN],
-                    rhs=g_codes[unit][:].bitcast(FP8X4),
-                    rhs_scale=g_scales[unit][:],
+                    rhs=g_codes[unit][:, cols].bitcast(FP8X4),
+                    rhs_scale=g_scales[unit][:, cols],
                     start=True,
                     stop=True,
                 )
                 y_banks.append(y_bank)
+            if first == 0:
+                product = glu.tile([P, HALF], F32, align_bytes=64)
+                gated[unit] = product
+            return y_banks
+
+        def gate(unit, y_banks, first=0, last=BLOCKS):
+            cols = slice(first * P, last * P)
             gate_bank, value_bank = y_banks
-            sig = glu.tile([P, HALF], F32)
+            sig = glu.tile([P, (last - first) * P], F32, tag="sig")
             nc.scalar.activation(
                 out=sig[:], in_=gate_bank[:], func=ACT.Sigmoid, bias=bias[:, 1:2], scale=1.0
             )
-            product = glu.tile([P, HALF], F32)
             nc.vector.scalar_tensor_tensor(
-                out=product[:],
+                out=gated[unit][:, cols],
                 in0=value_bank[:],
                 scalar=bias[:, 0:1],
                 in1=sig[:],
                 op0=ALU.add,
                 op1=ALU.mult,
             )
-            gated[unit] = product
 
-        def write_out(b):
-            t_banks = []
-            for half in range(HALVES):
-                t_bank = psum_t.tile([P, BLOCKS, HIDDEN], F32, tag="t")
-                for k in range(BLOCKS):
-                    nc.tensor.transpose(
-                        out=t_bank[:, k, :],
-                        in_=gated[HALVES * b + half][:, k * P : (k + 1) * P],
-                        identity=ident_f32[:],
-                    )
-                t_banks.append(t_bank)
-            for half in range(HALVES):
-                result = glu.tile([P, BLOCKS, HIDDEN], F32)
-                if half == 0:
-                    nc.vector.tensor_copy(out=result[:], in_=t_banks[half][:])
-                else:
-                    nc.scalar.copy(out=result[:], in_=t_banks[half][:])
-                nc.sync.dma_start(
-                    out=out[half * HALF : (half + 1) * HALF, b, :].rearrange("(k p) j -> p k j", p=P),
-                    in_=result[:],
+        def turn(unit, first=0, last=BLOCKS):
+            t_bank = psum_t.tile([P, last - first, HIDDEN], F32, tag="t")
+            for k in range(first, last):
+                nc.tensor.transpose(
+                    out=t_bank[:, k - first, :],
+                    in_=gated[unit][:, k * P : (k + 1) * P],
+                    identity=ident_f32[:],
                 )
+            return t_bank
+
+        def turn_blocks(unit):
+            b, half = divmod(unit, HALVES)
+            turned = glu.tile([P, HALF], F32, align_bytes=64)
+            nc.vector.transpose(out=turned[:], in_=gated[unit][:])
+            for J in range(HIDDEN // SQ):
+                rows = slice(J * SQ, (J + 1) * SQ)
+                nc.sync.dma_start(
+                    out=out[half * HALF : (half + 1) * HALF, b, rows].rearrange("(V v) j -> v V j", v=SQ),
+                    in_=turned[rows, :].rearrange("v (V j) -> v V j", j=SQ),
+                )
+
+        def store(unit, t_bank, engine, first=0, last=BLOCKS):
+            b, half = divmod(unit, HALVES)
+            result = glu.tile([P, last - first, HIDDEN], F32, tag="result")
+            copy(engine, result[:], t_bank[:])
+            rows = out[half * HALF + first * P : half * HALF + last * P, b, :]
+            nc.sync.dma_start(out=rows.rearrange("(k p) j -> p k j", p=P), in_=result[:])
 
         regroup_x(0)
         regroup_x(1)
@@ -260,16 +279,21 @@ def tile_stsgcm_pa_t_kernel(tc, x, A, W0, b0, out):
             prepare_a(half)
         regroup_x(2)
 
+        LAST = UNITS - 1
         for step in range(UNITS + 2):
             if step < UNITS:
-                stage1(step)
+                for k in range(BLOCKS):
+                    stage1(step, k, "S")
             if step + 2 < PIECES:
                 quantise_x(step + 2)
             if step + 3 < PIECES:
                 regroup_x(step + 3)
+            if 2 <= step < UNITS:
+                turn_blocks(step - 2)
             if step < UNITS:
                 quantise_g(step)
             if 1 <= step <= UNITS:
-                stage2(step - 1)
-            if step >= 3 and step % 2 == 1:
-                write_out((step - 3) // 2)
+                gate(step - 1, stage2(step - 1))
+        banks = [turn(LAST - 1), turn(LAST)]
+        store(LAST - 1, banks[0], "V")
+        store(LAST, banks[1], "S")

@@ -40,11 +40,10 @@ def tile_stsgcm_pa_t_kernel(tc, x, A, W0, b0, out):
         a_load = ctx.enter_context(tc.tile_pool(name="a_load", bufs=HALVES * BLOCKS))
         a_keep = ctx.enter_context(tc.tile_pool(name="a_keep", bufs=HALVES * BLOCKS))
         x_stage = ctx.enter_context(tc.tile_pool(name="x_stage", bufs=3))
-        g_stage = ctx.enter_context(tc.tile_pool(name="g_stage", bufs=3))
-        glu = ctx.enter_context(tc.tile_pool(name="glu", bufs=4))
+        g_stage = ctx.enter_context(tc.tile_pool(name="g_stage", bufs=4))
+        glu = ctx.enter_context(tc.tile_pool(name="glu", bufs=5))
         psum_g = ctx.enter_context(tc.psum_pool(name="psum_g", bufs=4))
-        psum_y = ctx.enter_context(tc.psum_pool(name="psum_y", bufs=2))
-        psum_t = ctx.enter_context(tc.psum_pool(name="psum_t", bufs=2))
+        psum_y = ctx.enter_context(tc.psum_pool(name="psum_y", bufs=4))
 
         ident_f32 = const.tile([P, P], F32)
         make_identity(nc, ident_f32[:])
@@ -89,7 +88,7 @@ def tile_stsgcm_pa_t_kernel(tc, x, A, W0, b0, out):
             )
         w_grouped = const.tile([P, 2 * HIDDEN, PACK], BF16, align_bytes=64)
         for h in range(2):
-            w_bank = psum_t.tile([P, PACK, P], BF16, tag="t")
+            w_bank = psum_y.tile([P, PACK, P], BF16, tag="y")
             for t in range(PACK):
                 nc.tensor.transpose(
                     out=w_bank[:, t, :], in_=w_slots[:, h, t, :], identity=ident_bf16[:]
@@ -167,7 +166,10 @@ def tile_stsgcm_pa_t_kernel(tc, x, A, W0, b0, out):
         g_grouped = {}
         g_codes = {}
         g_scales = {}
+        y_banks = {}
+        gates = {}
         gated = {}
+        turned_banks = {}
 
         def stage1(unit, k, engine):
             b, half = divmod(unit, HALVES)
@@ -209,7 +211,7 @@ def tile_stsgcm_pa_t_kernel(tc, x, A, W0, b0, out):
 
         def stage2(unit, first=0, last=BLOCKS, pool=psum_y, tag="y"):
             cols = slice(first * P, last * P)
-            y_banks = []
+            banks = []
             for h in (1, 0):
                 y_bank = pool.tile([P, (last - first) * P], F32, tag=tag)
                 nc.tensor.matmul_mx(
@@ -221,37 +223,39 @@ def tile_stsgcm_pa_t_kernel(tc, x, A, W0, b0, out):
                     start=True,
                     stop=True,
                 )
-                y_banks.append(y_bank)
-            if first == 0:
-                product = glu.tile([P, HALF], F32, align_bytes=64)
-                gated[unit] = product
-            return y_banks
+                banks.append(y_bank)
+            y_banks[unit, first] = banks
 
-        def gate(unit, y_banks, first=0, last=BLOCKS):
-            cols = slice(first * P, last * P)
-            gate_bank, value_bank = y_banks
+        def sigmoid(unit, first=0, last=BLOCKS):
+            gate_bank, value_bank = y_banks[unit, first]
             sig = glu.tile([P, (last - first) * P], F32, tag="sig")
             nc.scalar.activation(
                 out=sig[:], in_=gate_bank[:], func=ACT.Sigmoid, bias=bias[:, 1:2], scale=1.0
             )
+            gates[unit, first] = sig
+
+        def gate(unit, first=0, last=BLOCKS):
+            if first == 0:
+                product = glu.tile([P, HALF], F32, align_bytes=64)
+                gated[unit] = product
             nc.vector.scalar_tensor_tensor(
-                out=gated[unit][:, cols],
-                in0=value_bank[:],
+                out=gated[unit][:, first * P : last * P],
+                in0=y_banks[unit, first][1][:],
                 scalar=bias[:, 0:1],
-                in1=sig[:],
+                in1=gates[unit, first][:],
                 op0=ALU.add,
                 op1=ALU.mult,
             )
 
-        def turn(unit, first=0, last=BLOCKS):
-            t_bank = psum_t.tile([P, last - first, HIDDEN], F32, tag="t")
+        def turn(unit, first=0, last=BLOCKS, pool=psum_y, tag="y"):
+            t_bank = pool.tile([P, last - first, HIDDEN], F32, tag=tag)
             for k in range(first, last):
                 nc.tensor.transpose(
                     out=t_bank[:, k - first, :],
                     in_=gated[unit][:, k * P : (k + 1) * P],
                     identity=ident_f32[:],
                 )
-            return t_bank
+            turned_banks[unit, first] = t_bank
 
         def turn_blocks(unit):
             b, half = divmod(unit, HALVES)
@@ -264,13 +268,14 @@ def tile_stsgcm_pa_t_kernel(tc, x, A, W0, b0, out):
                     in_=turned[rows, :].rearrange("v (V j) -> v V j", j=SQ),
                 )
 
-        def store(unit, t_bank, engine, first=0, last=BLOCKS):
+        def store(unit, engine, first=0, last=BLOCKS):
             b, half = divmod(unit, HALVES)
             result = glu.tile([P, last - first, HIDDEN], F32, tag="result")
-            copy(engine, result[:], t_bank[:])
+            copy(engine, result[:], turned_banks[unit, first][:])
             rows = out[half * HALF + first * P : half * HALF + last * P, b, :]
             nc.sync.dma_start(out=rows.rearrange("(k p) j -> p k j", p=P), in_=result[:])
 
+        TENSOR_TURNS = (1, 3)
         regroup_x(0)
         regroup_x(1)
         quantise_x(0)
@@ -278,22 +283,65 @@ def tile_stsgcm_pa_t_kernel(tc, x, A, W0, b0, out):
         for half in range(HALVES):
             prepare_a(half)
         regroup_x(2)
+        regroup_x(3)
+        quantise_x(2)
 
-        LAST = UNITS - 1
-        for step in range(UNITS + 2):
-            if step < UNITS:
-                for k in range(BLOCKS):
-                    stage1(step, k, "S")
-            if step + 2 < PIECES:
-                quantise_x(step + 2)
+        for step in range(14):
+            for k in range(BLOCKS):
+                stage1(step, k, "S")
+            if step >= 2:
+                stage2(step - 2)
+                sigmoid(step - 2)
+            if step >= 5 and step % 2 == 1 and (step - 5) // 2 in TENSOR_TURNS:
+                turn(step - 5)
+                turn(step - 4)
+                store(step - 5, "S")
+                store(step - 4, "S")
+            if step >= 3:
+                gate(step - 3)
+            if step >= 1:
+                quantise_g(step - 1)
             if step + 3 < PIECES:
-                regroup_x(step + 3)
-            if 2 <= step < UNITS:
-                turn_blocks(step - 2)
-            if step < UNITS:
-                quantise_g(step)
-            if 1 <= step <= UNITS:
-                gate(step - 1, stage2(step - 1))
-        banks = [turn(LAST - 1), turn(LAST)]
-        store(LAST - 1, banks[0], "V")
-        store(LAST, banks[1], "S")
+                quantise_x(step + 3)
+            if step + 4 < PIECES:
+                regroup_x(step + 4)
+            if step >= 4 and (step - 4) // 2 not in TENSOR_TURNS:
+                turn_blocks(step - 4)
+
+        for k in range(BLOCKS):
+            stage1(14, k, "S")
+        stage2(12)
+        sigmoid(12)
+        quantise_g(13)
+        turn_blocks(10)
+        gate(11)
+        stage2(13)
+        sigmoid(13)
+        stage1(15, 0, "S")
+        stage1(15, 1, "S")
+        turn_blocks(11)
+        gate(12)
+        quantise_g(14)
+        stage1(15, 2, "V")
+        stage2(14)
+        stage1(15, 3, "S")
+        gate(13)
+        sigmoid(14)
+        quantise_g(15, 0, 2)
+        turn_blocks(12)
+        stage2(15, 0, 2)
+        turn(13, 0, 4, psum_g, "g")
+        quantise_g(15, 2, 4)
+        stage2(15, 2, 4)
+        sigmoid(15, 0, 2)
+        gate(14)
+        sigmoid(15, 2, 4)
+        gate(15, 0, 2)
+        store(13, "S")
+        turn(14, 0, 4, psum_g, "g")
+        turn(15, 0, 2, psum_g, "g")
+        gate(15, 2, 4)
+        store(14, "V")
+        turn(15, 2, 4, psum_g, "g")
+        store(15, "S", 0, 2)
+        store(15, "V", 2, 4)

@@ -39,9 +39,10 @@ def tile_stsgcm_pa_t_kernel(tc, x, A, W0, b0, out):
         x_keep = ctx.enter_context(tc.tile_pool(name="x_keep", bufs=PIECES))
         a_load = ctx.enter_context(tc.tile_pool(name="a_load", bufs=HALVES * BLOCKS))
         a_keep = ctx.enter_context(tc.tile_pool(name="a_keep", bufs=HALVES * BLOCKS))
-        x_stage = ctx.enter_context(tc.tile_pool(name="x_stage", bufs=3))
-        g_stage = ctx.enter_context(tc.tile_pool(name="g_stage", bufs=4))
-        glu = ctx.enter_context(tc.tile_pool(name="glu", bufs=5))
+        regrouped = ctx.enter_context(tc.tile_pool(name="regrouped", bufs=2))
+        quantised = ctx.enter_context(tc.tile_pool(name="quantised", bufs=3))
+        products = ctx.enter_context(tc.tile_pool(name="products", bufs=3))
+        glu = ctx.enter_context(tc.tile_pool(name="glu", bufs=4))
         psum_g = ctx.enter_context(tc.psum_pool(name="psum_g", bufs=4))
         psum_y = ctx.enter_context(tc.psum_pool(name="psum_y", bufs=4))
 
@@ -93,7 +94,7 @@ def tile_stsgcm_pa_t_kernel(tc, x, A, W0, b0, out):
                 nc.tensor.transpose(
                     out=w_bank[:, t, :], in_=w_slots[:, h, t, :], identity=ident_bf16[:]
                 )
-            nc.vector.tensor_copy(
+            nc.scalar.copy(
                 out=w_grouped[:, h * HIDDEN : (h + 1) * HIDDEN, :],
                 in_=w_bank[:].rearrange("p t o -> p o t"),
             )
@@ -103,36 +104,38 @@ def tile_stsgcm_pa_t_kernel(tc, x, A, W0, b0, out):
         nc.vector.tensor_copy(out=bias[:], in_=bias_bank[:, 0:2])
         w_codes = const.tile([P, 2 * HIDDEN], U32, align_bytes=64)
         w_scales = const.tile([P, 2 * HIDDEN], U8, align_bytes=64)
-        nc.vector.quantize_mx(
-            out=w_codes[:].bitcast(FP8X4),
-            scales=w_scales[:],
-            in_=w_grouped[:].rearrange("p o t -> p (o t)"),
-        )
+
+        def quantise_w():
+            nc.vector.quantize_mx(
+                out=w_codes[:].bitcast(FP8X4),
+                scales=w_scales[:],
+                in_=w_grouped[:].rearrange("p o t -> p (o t)"),
+            )
 
         x_grouped = {}
         x_codes = {}
         x_scales = {}
 
         def regroup_x(piece):
-            grouped = x_stage.tile([P, CHANNELS, PACK], BF16, align_bytes=64)
-            nc.vector.tensor_copy(
-                out=grouped[:].rearrange("p (t q i) j -> p t q j i", t=PACK, i=RUN),
-                in_=x_raw[piece][:].rearrange("p j (q t i) -> p t q j i", t=PACK, i=RUN),
-            )
-            x_grouped[piece] = grouped
-
-        def quantise_x(piece):
             b, s = divmod(piece, PASSES)
             if s == 0:
-                codes = x_stage.tile([P, PASSES, CHANNELS], U32, align_bytes=64)
-                scales = x_stage.tile([P, PASSES, CHANNELS], U8, align_bytes=64)
-                x_codes[b] = codes
-                x_scales[b] = scales
-            nc.vector.quantize_mx(
-                out=x_codes[b][:, s, :].bitcast(FP8X4),
-                scales=x_scales[b][:, s, :],
-                in_=x_grouped[piece][:].rearrange("p c t -> p (c t)"),
+                grouped = regrouped.tile([P, PASSES, CHANNELS, PACK], BF16, align_bytes=64, tag="x")
+                x_grouped[b] = grouped
+            nc.vector.tensor_copy(
+                out=x_grouped[b][:, s].rearrange("p (t q i) j -> p t q j i", t=PACK, i=RUN),
+                in_=x_raw[piece][:].rearrange("p j (q t i) -> p t q j i", t=PACK, i=RUN),
             )
+
+        def quantise_x(b):
+            codes = quantised.tile([P, PASSES, CHANNELS], U32, align_bytes=64, tag="x_codes")
+            scales = quantised.tile([P, PASSES, CHANNELS], U8, align_bytes=64, tag="x_scales")
+            nc.vector.quantize_mx(
+                out=codes[:].rearrange("p s c -> p (s c)").bitcast(FP8X4),
+                scales=scales[:].rearrange("p s c -> p (s c)"),
+                in_=x_grouped[b][:].rearrange("p s c j -> p (s c j)"),
+            )
+            x_codes[b] = codes
+            x_scales[b] = scales
 
         a_codes = {}
         a_scales = {}
@@ -173,9 +176,10 @@ def tile_stsgcm_pa_t_kernel(tc, x, A, W0, b0, out):
 
         def stage1(unit, k, engine):
             b, half = divmod(unit, HALVES)
-            if k == 0:
-                grouped = g_stage.tile([P, HALF, PACK], BF16, align_bytes=64)
-                g_grouped[unit] = grouped
+            if half == 0 and k == 0:
+                grouped = regrouped.tile([P, NODES, PACK], BF16, align_bytes=64, tag="g")
+                g_grouped[b] = grouped
+            first = (half * BLOCKS + k) * P
             g_bank = psum_g.tile([P, PACK, P], F32, tag="g")
             for t in range(PACK):
                 for s in range(PASSES):
@@ -188,7 +192,7 @@ def tile_stsgcm_pa_t_kernel(tc, x, A, W0, b0, out):
                         start=(s == 0),
                         stop=(s == PASSES - 1),
                     )
-            copy(engine, g_grouped[unit][:, k * P : (k + 1) * P, :], g_bank[:].rearrange("p t v -> p v t"))
+            copy(engine, g_grouped[b][:, first : first + P, :], g_bank[:].rearrange("p t v -> p v t"))
 
         def copy(engine, out_ap, in_ap):
             if engine == "V":
@@ -197,29 +201,31 @@ def tile_stsgcm_pa_t_kernel(tc, x, A, W0, b0, out):
                 nc.scalar.copy(out=out_ap, in_=in_ap)
 
         def quantise_g(unit, first=0, last=BLOCKS):
-            if first == 0:
-                codes = g_stage.tile([P, HALF], U32, align_bytes=64)
-                scales = g_stage.tile([P, HALF], U8, align_bytes=64)
-                g_codes[unit] = codes
-                g_scales[unit] = scales
-            cols = slice(first * P, last * P)
+            b, half = divmod(unit, HALVES)
+            if half == 0 and first == 0:
+                codes = quantised.tile([P, NODES], U32, align_bytes=64, tag="g_codes")
+                scales = quantised.tile([P, NODES], U8, align_bytes=64, tag="g_scales")
+                g_codes[b] = codes
+                g_scales[b] = scales
+            cols = slice(half * HALF + first * P, half * HALF + last * P)
             nc.vector.quantize_mx(
-                out=g_codes[unit][:, cols].bitcast(FP8X4),
-                scales=g_scales[unit][:, cols],
-                in_=g_grouped[unit][:, cols, :].rearrange("p v t -> p (v t)"),
+                out=g_codes[b][:, cols].bitcast(FP8X4),
+                scales=g_scales[b][:, cols],
+                in_=g_grouped[b][:, cols, :].rearrange("p v t -> p (v t)"),
             )
 
         def stage2(unit, first=0, last=BLOCKS, pool=psum_y, tag="y"):
-            cols = slice(first * P, last * P)
+            b, half = divmod(unit, HALVES)
+            cols = slice(half * HALF + first * P, half * HALF + last * P)
             banks = []
-            for h in (1, 0):
+            for h in range(2):
                 y_bank = pool.tile([P, (last - first) * P], F32, tag=tag)
                 nc.tensor.matmul_mx(
                     out=y_bank[:],
                     lhsT=w_codes[:, h * HIDDEN : (h + 1) * HIDDEN].bitcast(FP8X4),
                     lhsT_scale=w_scales[:, h * HIDDEN : (h + 1) * HIDDEN],
-                    rhs=g_codes[unit][:, cols].bitcast(FP8X4),
-                    rhs_scale=g_scales[unit][:, cols],
+                    rhs=g_codes[b][:, cols].bitcast(FP8X4),
+                    rhs_scale=g_scales[b][:, cols],
                     start=True,
                     stop=True,
                 )
@@ -227,7 +233,7 @@ def tile_stsgcm_pa_t_kernel(tc, x, A, W0, b0, out):
             y_banks[unit, first] = banks
 
         def sigmoid(unit, first=0, last=BLOCKS):
-            gate_bank, value_bank = y_banks[unit, first]
+            value_bank, gate_bank = y_banks[unit, first]
             sig = glu.tile([P, (last - first) * P], F32, tag="sig")
             nc.scalar.activation(
                 out=sig[:], in_=gate_bank[:], func=ACT.Sigmoid, bias=bias[:, 1:2], scale=1.0
@@ -235,12 +241,13 @@ def tile_stsgcm_pa_t_kernel(tc, x, A, W0, b0, out):
             gates[unit, first] = sig
 
         def gate(unit, first=0, last=BLOCKS):
-            if first == 0:
-                product = glu.tile([P, HALF], F32, align_bytes=64)
-                gated[unit] = product
+            b, half = divmod(unit, HALVES)
+            if half == 0 and first == 0:
+                product = products.tile([P, NODES], F32, align_bytes=64)
+                gated[b] = product
             nc.vector.scalar_tensor_tensor(
-                out=gated[unit][:, first * P : last * P],
-                in0=y_banks[unit, first][1][:],
+                out=gated[b][:, half * HALF + first * P : half * HALF + last * P],
+                in0=y_banks[unit, first][0][:],
                 scalar=bias[:, 0:1],
                 in1=gates[unit, first][:],
                 op0=ALU.add,
@@ -249,22 +256,23 @@ def tile_stsgcm_pa_t_kernel(tc, x, A, W0, b0, out):
 
         def turn(unit, first=0, last=BLOCKS, pool=psum_y, tag="y"):
             t_bank = pool.tile([P, last - first, HIDDEN], F32, tag=tag)
+            b, half = divmod(unit, HALVES)
             for k in range(first, last):
+                block = half * BLOCKS + k
                 nc.tensor.transpose(
                     out=t_bank[:, k - first, :],
-                    in_=gated[unit][:, k * P : (k + 1) * P],
+                    in_=gated[b][:, block * P : (block + 1) * P],
                     identity=ident_f32[:],
                 )
             turned_banks[unit, first] = t_bank
 
-        def turn_blocks(unit):
-            b, half = divmod(unit, HALVES)
-            turned = glu.tile([P, HALF], F32, align_bytes=64)
-            nc.vector.transpose(out=turned[:], in_=gated[unit][:])
+        def turn_blocks(b, first=0, last=NODES):
+            turned = products.tile([P, last - first], F32, align_bytes=64, tag="turned")
+            nc.vector.transpose(out=turned[:], in_=gated[b][:, first:last])
             for J in range(HIDDEN // SQ):
                 rows = slice(J * SQ, (J + 1) * SQ)
                 nc.sync.dma_start(
-                    out=out[half * HALF : (half + 1) * HALF, b, rows].rearrange("(V v) j -> v V j", v=SQ),
+                    out=out[first:last, b, rows].rearrange("(V v) j -> v V j", v=SQ),
                     in_=turned[rows, :].rearrange("v (V j) -> v V j", j=SQ),
                 )
 
@@ -275,51 +283,52 @@ def tile_stsgcm_pa_t_kernel(tc, x, A, W0, b0, out):
             rows = out[half * HALF + first * P : half * HALF + last * P, b, :]
             nc.sync.dma_start(out=rows.rearrange("(k p) j -> p k j", p=P), in_=result[:])
 
-        TENSOR_TURNS = (1, 3)
+        TENSOR_TURNS = (1, 2, 3)
         regroup_x(0)
         regroup_x(1)
+        quantise_w()
         quantise_x(0)
-        quantise_x(1)
         for half in range(HALVES):
             prepare_a(half)
         regroup_x(2)
-        regroup_x(3)
-        quantise_x(2)
 
         for step in range(14):
+            b, half = divmod(step, HALVES)
             for k in range(BLOCKS):
                 stage1(step, k, "S")
             if step >= 2:
                 stage2(step - 2)
                 sigmoid(step - 2)
-            if step >= 5 and step % 2 == 1 and (step - 5) // 2 in TENSOR_TURNS:
-                turn(step - 5)
-                turn(step - 4)
-                store(step - 5, "S")
-                store(step - 4, "S")
+            if half == 1 and b >= 2:
+                if b - 2 in TENSOR_TURNS:
+                    turn(step - 5)
+                    turn(step - 4)
+                    store(step - 5, "S")
+                    store(step - 4, "S")
+                else:
+                    turn_blocks(b - 2)
             if step >= 3:
                 gate(step - 3)
+            if half == 0:
+                regroup_x(step + 3)
             if step >= 1:
                 quantise_g(step - 1)
-            if step + 3 < PIECES:
-                quantise_x(step + 3)
-            if step + 4 < PIECES:
-                regroup_x(step + 4)
-            if step >= 4 and (step - 4) // 2 not in TENSOR_TURNS:
-                turn_blocks(step - 4)
+            if half == 0:
+                quantise_x(b + 1)
+            elif step + 3 < PIECES:
+                regroup_x(step + 3)
 
         for k in range(BLOCKS):
             stage1(14, k, "S")
         stage2(12)
         sigmoid(12)
         quantise_g(13)
-        turn_blocks(10)
         gate(11)
+        turn_blocks(5)
         stage2(13)
         sigmoid(13)
         stage1(15, 0, "S")
         stage1(15, 1, "S")
-        turn_blocks(11)
         gate(12)
         quantise_g(14)
         stage1(15, 2, "V")
@@ -328,7 +337,7 @@ def tile_stsgcm_pa_t_kernel(tc, x, A, W0, b0, out):
         gate(13)
         sigmoid(14)
         quantise_g(15, 0, 2)
-        turn_blocks(12)
+        turn_blocks(6, 0, 512)
         stage2(15, 0, 2)
         turn(13, 0, 4, psum_g, "g")
         quantise_g(15, 2, 4)

@@ -38,7 +38,7 @@ def tile_stsgcm_pa_t_kernel(tc, x, A, W0, b0, out):
         const = ctx.enter_context(tc.tile_pool(name="const", bufs=1))
         x_keep = ctx.enter_context(tc.tile_pool(name="x_keep", bufs=PIECES))
         a_load = ctx.enter_context(tc.tile_pool(name="a_load", bufs=HALVES * BLOCKS))
-        a_keep = ctx.enter_context(tc.tile_pool(name="a_keep", bufs=HALVES * BLOCKS))
+        a_keep = ctx.enter_context(tc.tile_pool(name="a_keep", bufs=HALVES * BLOCKS // 2))
         regrouped = ctx.enter_context(tc.tile_pool(name="regrouped", bufs=2))
         quantised = ctx.enter_context(tc.tile_pool(name="quantised", bufs=3))
         products = ctx.enter_context(tc.tile_pool(name="products", bufs=3))
@@ -101,7 +101,7 @@ def tile_stsgcm_pa_t_kernel(tc, x, A, W0, b0, out):
         bias_bank = psum_y.tile([P, P], BF16, tag="y")
         nc.tensor.transpose(out=bias_bank[:], in_=bias_rows[:], identity=ident_bf16[:])
         bias = const.tile([P, 2], F32)
-        nc.vector.tensor_copy(out=bias[:], in_=bias_bank[:, 0:2])
+        nc.scalar.copy(out=bias[:], in_=bias_bank[:, 0:2])
         w_codes = const.tile([P, 2 * HIDDEN], U32, align_bytes=64)
         w_scales = const.tile([P, 2 * HIDDEN], U8, align_bytes=64)
 
@@ -151,20 +151,26 @@ def tile_stsgcm_pa_t_kernel(tc, x, A, W0, b0, out):
                         in_=a_words[:, s * 2 * P + u : (s + 1) * 2 * P : 2],
                         identity=ident_f32[:],
                     )
-                a_grouped = a_keep.tile([P, PASSES * P * PACK], BF16, align_bytes=64)
+                pair, side = divmod(block, 2)
+                if side == 0:
+                    a_grouped = a_keep.tile([P, 2 * PASSES * P * PACK], BF16, align_bytes=64)
+                width = PASSES * P * PACK
                 nc.scalar.copy(
-                    out=a_grouped[:].bitcast(F32).rearrange("p (s v u) -> p s v u", s=PASSES, u=2),
+                    out=a_grouped[:, side * width : (side + 1) * width]
+                    .bitcast(F32)
+                    .rearrange("p (s v u) -> p s v u", s=PASSES, u=2),
                     in_=a_bank[:].rearrange("p (s u) v -> p s v u", u=2),
                 )
-                codes = a_keep.tile([P, PASSES, P], U32, align_bytes=64)
-                scales = a_keep.tile([P, PASSES, P], U8, align_bytes=64)
-                nc.vector.quantize_mx(
-                    out=codes[:].rearrange("p s v -> p (s v)").bitcast(FP8X4),
-                    scales=scales[:].rearrange("p s v -> p (s v)"),
-                    in_=a_grouped[:],
-                )
-                a_codes[block] = codes
-                a_scales[block] = scales
+                if side == 1:
+                    codes = a_keep.tile([P, 2, PASSES, P], U32, align_bytes=64)
+                    scales = a_keep.tile([P, 2, PASSES, P], U8, align_bytes=64)
+                    nc.vector.quantize_mx(
+                        out=codes[:].rearrange("p k s v -> p (k s v)").bitcast(FP8X4),
+                        scales=scales[:].rearrange("p k s v -> p (k s v)"),
+                        in_=a_grouped[:],
+                    )
+                    a_codes[pair] = codes
+                    a_scales[pair] = scales
 
         g_grouped = {}
         g_codes = {}
@@ -180,6 +186,7 @@ def tile_stsgcm_pa_t_kernel(tc, x, A, W0, b0, out):
                 grouped = regrouped.tile([P, NODES, PACK], BF16, align_bytes=64, tag="g")
                 g_grouped[b] = grouped
             first = (half * BLOCKS + k) * P
+            pair, side = divmod(half * BLOCKS + k, 2)
             g_bank = psum_g.tile([P, PACK, P], F32, tag="g")
             for t in range(PACK):
                 for s in range(PASSES):
@@ -187,8 +194,8 @@ def tile_stsgcm_pa_t_kernel(tc, x, A, W0, b0, out):
                         out=g_bank[:, t, :],
                         lhsT=x_codes[b][:, s, t * P : (t + 1) * P].bitcast(FP8X4),
                         lhsT_scale=x_scales[b][:, s, t * P : (t + 1) * P],
-                        rhs=a_codes[half * BLOCKS + k][:, s, :].bitcast(FP8X4),
-                        rhs_scale=a_scales[half * BLOCKS + k][:, s, :],
+                        rhs=a_codes[pair][:, side, s, :].bitcast(FP8X4),
+                        rhs_scale=a_scales[pair][:, side, s, :],
                         start=(s == 0),
                         stop=(s == PASSES - 1),
                     )
@@ -325,32 +332,32 @@ def tile_stsgcm_pa_t_kernel(tc, x, A, W0, b0, out):
         quantise_g(13)
         gate(11)
         turn_blocks(5)
+        stage1(15, 0, "S")
         stage2(13)
         sigmoid(13)
-        stage1(15, 0, "S")
-        stage1(15, 1, "S")
         gate(12)
         quantise_g(14)
-        stage1(15, 2, "V")
-        stage2(14)
-        stage1(15, 3, "S")
+        stage1(15, 1, "S")
+        stage1(15, 2, "S")
         gate(13)
-        sigmoid(14)
         quantise_g(15, 0, 2)
-        turn_blocks(6, 0, 512)
-        stage2(15, 0, 2)
-        turn(13, 0, 4, psum_g, "g")
+        stage1(15, 3, "S")
+        turn_blocks(6, 0, HALF)
+        stage2(14)
+        sigmoid(14)
         quantise_g(15, 2, 4)
+        turn(13, 0, 4, psum_g, "g")
+        stage2(15, 0, 2)
         stage2(15, 2, 4)
-        sigmoid(15, 0, 2)
         gate(14)
+        sigmoid(15, 0, 2)
+        store(13, "S")
         sigmoid(15, 2, 4)
         gate(15, 0, 2)
-        store(13, "S")
         turn(14, 0, 4, psum_g, "g")
-        turn(15, 0, 2, psum_g, "g")
         gate(15, 2, 4)
-        store(14, "V")
+        turn(15, 0, 2, psum_g, "g")
+        store(15, "V", 0, 2)
         turn(15, 2, 4, psum_g, "g")
-        store(15, "S", 0, 2)
+        store(14, "S")
         store(15, "V", 2, 4)

@@ -57,60 +57,41 @@ def tile_stsgcm_pa_t_kernel(tc, x, A, W0, b0, out):
         half_col = const.tile([P, 1], F32)
         nc.scalar.activation(out=half_col[:], in_=zero_col[:], func=ACT.Sigmoid)
 
-        w_raw = const.tile([P, 2, CHANNELS], BF16)
-        nc.sync.dma_start(out=w_raw[:], in_=W0.rearrange("(h o) c -> o h c", h=2))
-        nc.sync.dma_start(out=bias_rows[0:2, :], in_=b0.rearrange("(h j) -> h j", h=2))
+        zeros = const.tile([P, HALF], BF16)
+        nc.vector.memset(zeros[:], 0.0)
+        warm_bank = psum_y.tile([P, HALF], F32, tag="y")
+
+        def warm_up(times):
+            for _ in range(times):
+                nc.tensor.matmul(
+                    out=warm_bank[:], lhsT=zeros[:, 0:P], rhs=zeros[:], start=True, stop=True
+                )
+
+        warm_up(8)
 
         x_raw = {}
 
-        def load_x(b):
-            for s in range(PASSES):
-                x_piece = x_keep.tile([P, PACK, CHANNELS], BF16)
-                nc.sync.dma_start(
-                    out=x_piece[:],
-                    in_=x[s * P * PACK : (s + 1) * P * PACK, b, :].rearrange("(p t) c -> p t c", t=PACK),
-                )
-                x_raw[PASSES * b + s] = x_piece
+        def load_x(piece):
+            b, s = divmod(piece, PASSES)
+            x_piece = x_keep.tile([P, PACK, CHANNELS], BF16)
+            nc.sync.dma_start(
+                out=x_piece[:],
+                in_=x[s * P * PACK : (s + 1) * P * PACK, b, :].rearrange("(p t) c -> p t c", t=PACK),
+            )
+            x_raw[piece] = x_piece
 
         load_x(0)
+        w_raw = const.tile([P, 2, CHANNELS], BF16)
+        nc.sync.dma_start(out=w_raw[:], in_=W0.rearrange("(h o) c -> o h c", h=2))
+        nc.sync.dma_start(out=bias_rows[0:2, :], in_=b0.rearrange("(h j) -> h j", h=2))
+        load_x(1)
         a_raw = []
         for block in range(HALVES * BLOCKS):
             a_rows = a_load.tile([P, NODES], BF16)
             nc.sync.dma_start(out=a_rows[:], in_=A[block * P : (block + 1) * P, :])
             a_raw.append(a_rows)
-        for b in range(1, BATCH):
-            load_x(b)
-
-        w_slots = const.tile([P, 2, PACK, P], BF16)
-        for h in range(2):
-            nc.vector.tensor_copy(
-                out=w_slots[:, h].rearrange("p t (q i) -> p t q i", i=RUN),
-                in_=w_raw[:, h].rearrange("p (q t i) -> p t q i", t=PACK, i=RUN),
-            )
-        w_grouped = const.tile([P, 2 * HIDDEN, PACK], BF16, align_bytes=64)
-        for h in range(2):
-            w_bank = psum_y.tile([P, PACK, P], BF16, tag="y")
-            for t in range(PACK):
-                nc.tensor.transpose(
-                    out=w_bank[:, t, :], in_=w_slots[:, h, t, :], identity=ident_bf16[:]
-                )
-            nc.scalar.copy(
-                out=w_grouped[:, h * HIDDEN : (h + 1) * HIDDEN, :],
-                in_=w_bank[:].rearrange("p t o -> p o t"),
-            )
-        bias_bank = psum_y.tile([P, P], BF16, tag="y")
-        nc.tensor.transpose(out=bias_bank[:], in_=bias_rows[:], identity=ident_bf16[:])
-        bias = const.tile([P, 2], F32)
-        nc.scalar.copy(out=bias[:], in_=bias_bank[:, 0:2])
-        w_codes = const.tile([P, 2 * HIDDEN], U32, align_bytes=64)
-        w_scales = const.tile([P, 2 * HIDDEN], U8, align_bytes=64)
-
-        def quantise_w():
-            nc.vector.quantize_mx(
-                out=w_codes[:].bitcast(FP8X4),
-                scales=w_scales[:],
-                in_=w_grouped[:].rearrange("p o t -> p (o t)"),
-            )
+        for piece in range(PASSES, PIECES):
+            load_x(piece)
 
         x_grouped = {}
         x_codes = {}
@@ -137,6 +118,41 @@ def tile_stsgcm_pa_t_kernel(tc, x, A, W0, b0, out):
             x_codes[b] = codes
             x_scales[b] = scales
 
+        regroup_x(0)
+
+        w_slots = const.tile([P, 2, PACK, P], BF16)
+        for h in range(2):
+            nc.vector.tensor_copy(
+                out=w_slots[:, h].rearrange("p t (q i) -> p t q i", i=RUN),
+                in_=w_raw[:, h].rearrange("p (q t i) -> p t q i", t=PACK, i=RUN),
+            )
+        w_grouped = const.tile([P, 2 * HIDDEN, PACK], BF16, align_bytes=64)
+        for h in range(2):
+            w_bank = psum_y.tile([P, PACK, P], BF16, tag="y")
+            for t in range(PACK):
+                nc.tensor.transpose(
+                    out=w_bank[:, t, :], in_=w_slots[:, h, t, :], identity=ident_bf16[:]
+                )
+            nc.scalar.copy(
+                out=w_grouped[:, h * HIDDEN : (h + 1) * HIDDEN, :],
+                in_=w_bank[:].rearrange("p t o -> p o t"),
+            )
+        bias_bank = psum_y.tile([P, P], BF16, tag="y")
+        nc.tensor.transpose(out=bias_bank[:], in_=bias_rows[:], identity=ident_bf16[:])
+        bias = const.tile([P, 2], F32)
+        nc.scalar.copy(out=bias[:], in_=bias_bank[:, 0:2])
+        w_codes = const.tile([P, 2 * HIDDEN], U32, align_bytes=64)
+        w_scales = const.tile([P, 2 * HIDDEN], U8, align_bytes=64)
+
+        warm_up(4)
+
+        def quantise_w():
+            nc.vector.quantize_mx(
+                out=w_codes[:].bitcast(FP8X4),
+                scales=w_scales[:],
+                in_=w_grouped[:].rearrange("p o t -> p (o t)"),
+            )
+
         a_codes = {}
         a_scales = {}
 
@@ -161,6 +177,8 @@ def tile_stsgcm_pa_t_kernel(tc, x, A, W0, b0, out):
                     .rearrange("p (s v u) -> p s v u", s=PASSES, u=2),
                     in_=a_bank[:].rearrange("p (s u) v -> p s v u", u=2),
                 )
+                if side == 1:
+                    warm_up(1)
                 if side == 1:
                     codes = a_keep.tile([P, 2, PASSES, P], U32, align_bytes=64)
                     scales = a_keep.tile([P, 2, PASSES, P], U8, align_bytes=64)
@@ -291,7 +309,6 @@ def tile_stsgcm_pa_t_kernel(tc, x, A, W0, b0, out):
             nc.sync.dma_start(out=rows.rearrange("(k p) j -> p k j", p=P), in_=result[:])
 
         TENSOR_TURNS = (1, 2, 3)
-        regroup_x(0)
         regroup_x(1)
         quantise_w()
         quantise_x(0)

@@ -308,7 +308,7 @@ def tile_stsgcm_pa_t_kernel(tc, x, A, W0, b0, out):
             rows = out[half * HALF + first * P : half * HALF + last * P, b, :]
             nc.sync.dma_start(out=rows.rearrange("(k p) j -> p k j", p=P), in_=result[:])
 
-        TENSOR_TURNS = (1, 2, 3)
+        TENSOR_TURNS = (1, 3)
         regroup_x(1)
         quantise_w()
         quantise_x(0)

@@ -108,8 +108,8 @@ def tile_stsgcm_pa_t_kernel(tc, x, A, W0, b0, out):
             )
 
         def quantise_x(b):
-            codes = quantised.tile([P, PASSES, CHANNELS], U32, align_bytes=64, tag="x_codes")
-            scales = quantised.tile([P, PASSES, CHANNELS], U8, align_bytes=64, tag="x_scales")
+            codes = quantised.tile([P, PASSES, CHANNELS], U32, align_bytes=256, tag="x_codes")
+            scales = quantised.tile([P, PASSES, CHANNELS], U8, align_bytes=256, tag="x_scales")
             nc.vector.quantize_mx(
                 out=codes[:].rearrange("p s c -> p (s c)").bitcast(FP8X4),
                 scales=scales[:].rearrange("p s c -> p (s c)"),
@@ -141,8 +141,8 @@ def tile_stsgcm_pa_t_kernel(tc, x, A, W0, b0, out):
         nc.tensor.transpose(out=bias_bank[:], in_=bias_rows[:], identity=ident_bf16[:])
         bias = const.tile([P, 2], F32)
         nc.scalar.copy(out=bias[:], in_=bias_bank[:, 0:2])
-        w_codes = const.tile([P, 2 * HIDDEN], U32, align_bytes=64)
-        w_scales = const.tile([P, 2 * HIDDEN], U8, align_bytes=64)
+        w_codes = const.tile([P, 2 * HIDDEN], U32, align_bytes=256)
+        w_scales = const.tile([P, 2 * HIDDEN], U8, align_bytes=256)
 
         warm_up(4)
 
@@ -180,8 +180,8 @@ def tile_stsgcm_pa_t_kernel(tc, x, A, W0, b0, out):
                 if side == 1:
                     warm_up(1)
                 if side == 1:
-                    codes = a_keep.tile([P, 2, PASSES, P], U32, align_bytes=64)
-                    scales = a_keep.tile([P, 2, PASSES, P], U8, align_bytes=64)
+                    codes = a_keep.tile([P, 2, PASSES, P], U32, align_bytes=256)
+                    scales = a_keep.tile([P, 2, PASSES, P], U8, align_bytes=256)
                     nc.vector.quantize_mx(
                         out=codes[:].rearrange("p k s v -> p (k s v)").bitcast(FP8X4),
                         scales=scales[:].rearrange("p k s v -> p (k s v)"),
@@ -228,8 +228,8 @@ def tile_stsgcm_pa_t_kernel(tc, x, A, W0, b0, out):
         def quantise_g(unit, first=0, last=BLOCKS):
             b, half = divmod(unit, HALVES)
             if half == 0 and first == 0:
-                codes = quantised.tile([P, NODES], U32, align_bytes=64, tag="g_codes")
-                scales = quantised.tile([P, NODES], U8, align_bytes=64, tag="g_scales")
+                codes = quantised.tile([P, NODES], U32, align_bytes=256, tag="g_codes")
+                scales = quantised.tile([P, NODES], U8, align_bytes=256, tag="g_scales")
                 g_codes[b] = codes
                 g_scales[b] = scales
             cols = slice(half * HALF + first * P, half * HALF + last * P)

from contextlib import ExitStack

import concourse.mybir as mybir
from concourse.masks import make_identity

F32 = mybir.dt.float32
BF16 = mybir.dt.bfloat16
U32 = mybir.dt.uint32
U8 = mybir.dt.uint8
FP8X4 = mybir.dt.float8_e4m3fn_x4
ACT = mybir.ActivationFunctionType
ALU = mybir.AluOpType

P = 128
PACK = 4
SQ = 32
RUN = 8
NODES = 1024
BATCH = 8
CHANNELS = 512
HIDDEN = 128

PASSES = NODES // (P * PACK)
HALF = 512
HALVES = NODES // HALF
BLOCKS = HALF // P
UNITS = BATCH * HALVES
PIECES = BATCH * PASSES

FLOPS = 2 * BATCH * CHANNELS * NODES * NODES + 2 * BATCH * 2 * HIDDEN * CHANNELS * NODES


def tile_stsgcm_pa_t_kernel(tc, x, A, W0, b0, out):
    nc = tc.nc
    with ExitStack() as ctx:
        ctx.enter_context(tc.manual_schedule())

        const = ctx.enter_context(tc.tile_pool(name="const", bufs=1))
        x_keep = ctx.enter_context(tc.tile_pool(name="x_keep", bufs=PIECES))
        a_load = ctx.enter_context(tc.tile_pool(name="a_load", bufs=HALVES * BLOCKS))
        a_keep = ctx.enter_context(tc.tile_pool(name="a_keep", bufs=HALVES * BLOCKS // 2))
        regrouped = ctx.enter_context(tc.tile_pool(name="regrouped", bufs=2))
        quantised = ctx.enter_context(tc.tile_pool(name="quantised", bufs=3))
        products = ctx.enter_context(tc.tile_pool(name="products", bufs=3))
        glu = ctx.enter_context(tc.tile_pool(name="glu", bufs=4))
        psum_g = ctx.enter_context(tc.psum_pool(name="psum_g", bufs=4))
        psum_y = ctx.enter_context(tc.psum_pool(name="psum_y", bufs=4))

        ident_f32 = const.tile([P, P], F32)
        make_identity(nc, ident_f32[:])
        ident_bf16 = const.tile([P, P], BF16)
        make_identity(nc, ident_bf16[:])
        bias_rows = const.tile([P, P], BF16)
        nc.vector.memset(bias_rows[:], 0.0)
        zero_col = const.tile([P, 1], F32)
        nc.vector.memset(zero_col[:], 0.0)
        half_col = const.tile([P, 1], F32)
        nc.scalar.activation(out=half_col[:], in_=zero_col[:], func=ACT.Sigmoid)

        zeros = const.tile([P, HALF], BF16)
        nc.vector.memset(zeros[:], 0.0)
        warm_bank = psum_y.tile([P, HALF], F32, tag="y")

        def warm_up(times):
            for _ in range(times):
                nc.tensor.matmul(
                    out=warm_bank[:], lhsT=zeros[:, 0:P], rhs=zeros[:], start=True, stop=True
                )

        warm_up(8)

        x_raw = {}

        def load_x(piece):
            b, s = divmod(piece, PASSES)
            x_piece = x_keep.tile([P, PACK, CHANNELS], BF16)
            nc.sync.dma_start(
                out=x_piece[:],
                in_=x[s * P * PACK : (s + 1) * P * PACK, b, :].rearrange("(p t) c -> p t c", t=PACK),
            )
            x_raw[piece] = x_piece

        load_x(0)
        w_raw = const.tile([P, 2, CHANNELS], BF16)
        nc.sync.dma_start(out=w_raw[:], in_=W0.rearrange("(h o) c -> o h c", h=2))
        nc.sync.dma_start(out=bias_rows[0:2, :], in_=b0.rearrange("(h j) -> h j", h=2))
        load_x(1)
        a_raw = []
        for block in range(HALVES * BLOCKS):
            a_rows = a_load.tile([P, NODES], BF16)
            nc.sync.dma_start(out=a_rows[:], in_=A[block * P : (block + 1) * P, :])
            a_raw.append(a_rows)
        for piece in range(PASSES, PIECES):
            load_x(piece)

        x_grouped = {}
        x_codes = {}
        x_scales = {}

        def regroup_x(piece):
            b, s = divmod(piece, PASSES)
            if s == 0:
                grouped = regrouped.tile([P, PASSES, CHANNELS, PACK], BF16, align_bytes=64, tag="x")
                x_grouped[b] = grouped
            nc.vector.tensor_copy(
                out=x_grouped[b][:, s].rearrange("p (t q i) j -> p t q j i", t=PACK, i=RUN),
                in_=x_raw[piece][:].rearrange("p j (q t i) -> p t q j i", t=PACK, i=RUN),
            )

        def quantise_x(b):
            codes = quantised.tile([P, PASSES, CHANNELS], U32, align_bytes=256, tag="x_codes")
            scales = quantised.tile([P, PASSES, CHANNELS], U8, align_bytes=256, tag="x_scales")
            nc.vector.quantize_mx(
                out=codes[:].rearrange("p s c -> p (s c)").bitcast(FP8X4),
                scales=scales[:].rearrange("p s c -> p (s c)"),
                in_=x_grouped[b][:].rearrange("p s c j -> p (s c j)"),
            )
            x_codes[b] = codes
            x_scales[b] = scales

        regroup_x(0)

        w_slots = const.tile([P, 2, PACK, P], BF16)
        for h in range(2):
            nc.vector.tensor_copy(
                out=w_slots[:, h].rearrange("p t (q i) -> p t q i", i=RUN),
                in_=w_raw[:, h].rearrange("p (q t i) -> p t q i", t=PACK, i=RUN),
            )
        w_grouped = const.tile([P, 2 * HIDDEN, PACK], BF16, align_bytes=64)
        for h in range(2):
            w_bank = psum_y.tile([P, PACK, P], BF16, tag="y")
            for t in range(PACK):
                nc.tensor.transpose(
                    out=w_bank[:, t, :], in_=w_slots[:, h, t, :], identity=ident_bf16[:]
                )
            nc.scalar.copy(
                out=w_grouped[:, h * HIDDEN : (h + 1) * HIDDEN, :],
                in_=w_bank[:].rearrange("p t o -> p o t"),
            )
        bias_bank = psum_y.tile([P, P], BF16, tag="y")
        nc.tensor.transpose(out=bias_bank[:], in_=bias_rows[:], identity=ident_bf16[:])
        bias = const.tile([P, 2], F32)
        nc.scalar.copy(out=bias[:], in_=bias_bank[:, 0:2])
        w_codes = const.tile([P, 2 * HIDDEN], U32, align_bytes=256)
        w_scales = const.tile([P, 2 * HIDDEN], U8, align_bytes=256)

        warm_up(4)

        def quantise_w():
            nc.vector.quantize_mx(
                out=w_codes[:].bitcast(FP8X4),
                scales=w_scales[:],
                in_=w_grouped[:].rearrange("p o t -> p (o t)"),
            )

        a_codes = {}
        a_scales = {}

        def prepare_a(half):
            for block in range(half * BLOCKS, (half + 1) * BLOCKS):
                a_words = a_raw[block][:].bitcast(F32)
                a_bank = psum_g.tile([P, PASSES * 2, P], F32, tag="g")
                for su in range(PASSES * 2):
                    s, u = divmod(su, 2)
                    nc.tensor.transpose(
                        out=a_bank[:, su, :],
                        in_=a_words[:, s * 2 * P + u : (s + 1) * 2 * P : 2],
                        identity=ident_f32[:],
                    )
                pair, side = divmod(block, 2)
                if side == 0:
                    a_grouped = a_keep.tile([P, 2 * PASSES * P * PACK], BF16, align_bytes=64)
                width = PASSES * P * PACK
                nc.scalar.copy(
                    out=a_grouped[:, side * width : (side + 1) * width]
                    .bitcast(F32)
                    .rearrange("p (s v u) -> p s v u", s=PASSES, u=2),
                    in_=a_bank[:].rearrange("p (s u) v -> p s v u", u=2),
                )
                if side == 1:
                    warm_up(1)
                if side == 1:
                    codes = a_keep.tile([P, 2, PASSES, P], U32, align_bytes=256)
                    scales = a_keep.tile([P, 2, PASSES, P], U8, align_bytes=256)
                    nc.vector.quantize_mx(
                        out=codes[:].rearrange("p k s v -> p (k s v)").bitcast(FP8X4),
                        scales=scales[:].rearrange("p k s v -> p (k s v)"),
                        in_=a_grouped[:],
                    )
                    a_codes[pair] = codes
                    a_scales[pair] = scales

        g_grouped = {}
        g_codes = {}
        g_scales = {}
        y_banks = {}
        gates = {}
        gated = {}
        turned_banks = {}

        def stage1(unit, k, engine):
            b, half = divmod(unit, HALVES)
            if half == 0 and k == 0:
                grouped = regrouped.tile([P, NODES, PACK], BF16, align_bytes=64, tag="g")
                g_grouped[b] = grouped
            first = (half * BLOCKS + k) * P
            pair, side = divmod(half * BLOCKS + k, 2)
            g_bank = psum_g.tile([P, PACK, P], F32, tag="g")
            for t in range(PACK):
                for s in range(PASSES):
                    nc.tensor.matmul_mx(
                        out=g_bank[:, t, :],
                        lhsT=x_codes[b][:, s, t * P : (t + 1) * P].bitcast(FP8X4),
                        lhsT_scale=x_scales[b][:, s, t * P : (t + 1) * P],
                        rhs=a_codes[pair][:, side, s, :].bitcast(FP8X4),
                        rhs_scale=a_scales[pair][:, side, s, :],
                        start=(s == 0),
                        stop=(s == PASSES - 1),
                    )
            copy(engine, g_grouped[b][:, first : first + P, :], g_bank[:].rearrange("p t v -> p v t"))

        def copy(engine, out_ap, in_ap):
            if engine == "V":
                nc.vector.tensor_copy(out=out_ap, in_=in_ap)
            else:
                nc.scalar.copy(out=out_ap, in_=in_ap)

        def quantise_g(unit, first=0, last=BLOCKS):
            b, half = divmod(unit, HALVES)
            if half == 0 and first == 0:
                codes = quantised.tile([P, NODES], U32, align_bytes=256, tag="g_codes")
                scales = quantised.tile([P, NODES], U8, align_bytes=256, tag="g_scales")
                g_codes[b] = codes
                g_scales[b] = scales
            cols = slice(half * HALF + first * P, half * HALF + last * P)
            nc.vector.quantize_mx(
                out=g_codes[b][:, cols].bitcast(FP8X4),
                scales=g_scales[b][:, cols],
                in_=g_grouped[b][:, cols, :].rearrange("p v t -> p (v t)"),
            )

        def stage2(unit, first=0, last=BLOCKS, pool=psum_y, tag="y"):
            b, half = divmod(unit, HALVES)
            cols = slice(half * HALF + first * P, half * HALF + last * P)
            banks = []
            for h in range(2):
                y_bank = pool.tile([P, (last - first) * P], F32, tag=tag)
                nc.tensor.matmul_mx(
                    out=y_bank[:],
                    lhsT=w_codes[:, h * HIDDEN : (h + 1) * HIDDEN].bitcast(FP8X4),
                    lhsT_scale=w_scales[:, h * HIDDEN : (h + 1) * HIDDEN],
                    rhs=g_codes[b][:, cols].bitcast(FP8X4),
                    rhs_scale=g_scales[b][:, cols],
                    start=True,
                    stop=True,
                )
                banks.append(y_bank)
            y_banks[unit, first] = banks

        def sigmoid(unit, first=0, last=BLOCKS):
            value_bank, gate_bank = y_banks[unit, first]
            sig = glu.tile([P, (last - first) * P], F32, tag="sig")
            nc.scalar.activation(
                out=sig[:], in_=gate_bank[:], func=ACT.Sigmoid, bias=bias[:, 1:2], scale=1.0
            )
            gates[unit, first] = sig

        def gate(unit, first=0, last=BLOCKS):
            b, half = divmod(unit, HALVES)
            if half == 0 and first == 0:
                product = products.tile([P, NODES], F32, align_bytes=64)
                gated[b] = product
            nc.vector.scalar_tensor_tensor(
                out=gated[b][:, half * HALF + first * P : half * HALF + last * P],
                in0=y_banks[unit, first][0][:],
                scalar=bias[:, 0:1],
                in1=gates[unit, first][:],
                op0=ALU.add,
                op1=ALU.mult,
            )

        def turn(unit, first=0, last=BLOCKS, pool=psum_y, tag="y"):
            t_bank = pool.tile([P, last - first, HIDDEN], F32, tag=tag)
            b, half = divmod(unit, HALVES)
            for k in range(first, last):
                block = half * BLOCKS + k
                nc.tensor.transpose(
                    out=t_bank[:, k - first, :],
                    in_=gated[b][:, block * P : (block + 1) * P],
                    identity=ident_f32[:],
                )
            turned_banks[unit, first] = t_bank

        def turn_blocks(b, first=0, last=NODES):
            turned = products.tile([P, last - first], F32, align_bytes=64, tag="turned")
            nc.vector.transpose(out=turned[:], in_=gated[b][:, first:last])
            for J in range(HIDDEN // SQ):
                rows = slice(J * SQ, (J + 1) * SQ)
                nc.sync.dma_start(
                    out=out[first:last, b, rows].rearrange("(V v) j -> v V j", v=SQ),
                    in_=turned[rows, :].rearrange("v (V j) -> v V j", j=SQ),
                )

        def store(unit, engine, first=0, last=BLOCKS):
            b, half = divmod(unit, HALVES)
            result = glu.tile([P, last - first, HIDDEN], F32, tag="result")
            copy(engine, result[:], turned_banks[unit, first][:])
            rows = out[half * HALF + first * P : half * HALF + last * P, b, :]
            nc.sync.dma_start(out=rows.rearrange("(k p) j -> p k j", p=P), in_=result[:])

        TENSOR_TURNS = (1, 3)
        regroup_x(1)
        quantise_w()
        quantise_x(0)
        for half in range(HALVES):
            prepare_a(half)
        regroup_x(2)

        for step in range(14):
            b, half = divmod(step, HALVES)
            for k in range(BLOCKS):
                stage1(step, k, "S")
            if step >= 2:
                stage2(step - 2)
                sigmoid(step - 2)
            if half == 1 and b >= 2:
                if b - 2 in TENSOR_TURNS:
                    turn(step - 5)
                    turn(step - 4)
                    store(step - 5, "S")
                    store(step - 4, "S")
                else:
                    turn_blocks(b - 2)
            if step >= 3:
                gate(step - 3)
            if half == 0:
                regroup_x(step + 3)
            if step >= 1:
                quantise_g(step - 1)
            if half == 0:
                quantise_x(b + 1)
            elif step + 3 < PIECES:
                regroup_x(step + 3)

        for k in range(BLOCKS):
            stage1(14, k, "S")
        stage2(12)
        sigmoid(12)
        quantise_g(13)
        gate(11)
        turn_blocks(5)
        stage1(15, 0, "S")
        stage2(13)
        sigmoid(13)
        gate(12)
        quantise_g(14)
        stage1(15, 1, "S")
        stage1(15, 2, "S")
        gate(13)
        quantise_g(15, 0, 2)
        stage1(15, 3, "S")
        turn_blocks(6, 0, HALF)
        stage2(14)
        sigmoid(14)
        quantise_g(15, 2, 4)
        turn(13, 0, 4, psum_g, "g")
        stage2(15, 0, 2)
        stage2(15, 2, 4)
        gate(14)
        sigmoid(15, 0, 2)
        store(13, "S")
        sigmoid(15, 2, 4)
        gate(15, 0, 2)
        turn(14, 0, 4, psum_g, "g")
        gate(15, 2, 4)
        turn(15, 0, 2, psum_g, "g")
        store(15, "V", 0, 2)
        turn(15, 2, 4, psum_g, "g")
        store(14, "S")
        store(15, "V", 2, 4)
